import numpy as np
import ml_dtypes


def mxq(x, axis, fmt="e4m3"):
    dtype, down = {"e4m3": (ml_dtypes.float8_e4m3fn, 7), "e5m2": (ml_dtypes.float8_e5m2, 14)}[fmt]
    v = np.moveaxis(np.asarray(x, np.float32).astype(ml_dtypes.bfloat16).astype(np.float64), axis, -1)
    blocks = v.reshape(v.shape[:-1] + (-1, 32))
    amax = np.abs(blocks).max(-1, keepdims=True)
    byte = np.maximum(np.where(amax > 0, np.frexp(amax)[1] - 1 + 127, 0) - down, 1)
    scale = np.exp2(byte - 127.0)
    codes = (blocks / scale).astype(np.float32).astype(dtype).astype(np.float64)
    return np.moveaxis((codes * scale).reshape(v.shape), -1, axis)


WIDE = False


def mx_kscale(k):
    if not WIDE:
        return np.ones(k)
    levels = np.array([10, -10, 5, -5, 0])
    a = np.random.permutation(np.resize(levels, k // 512 * 4)).reshape(k // 512, 4)
    idx = np.arange(k)
    return np.exp2(a[idx // 512, idx % 128 // 32])


BF16 = ml_dtypes.bfloat16


def bf(x):
    return np.asarray(x, np.float32).astype(BF16)


def f64(x):
    return np.asarray(x).astype(np.float64)


E2M1 = np.array([0.0, 0.5, 1.0, 1.5, 2.0, 3.0, 4.0, 6.0, -0.0, -0.5, -1.0, -1.5, -2.0, -3.0, -4.0, -6.0])


def pack_weight(w, fmt):
    k, n = w.shape
    w = f64(bf(w)).reshape(k // 32, 32, n)
    amax = np.abs(w).max(1)
    if fmt == "e4m3":
        byte = np.frexp(amax)[1] - 1 + 127 - 7
    else:
        mant, ex = np.frexp(amax / 6.0)
        byte = np.where(mant > 0.5, ex, ex - 1) + 127
    byte = np.clip(np.where(amax > 0, byte, 1), 1, 254)
    scaled = (w * np.exp2(127.0 - byte)[:, None, :]).reshape(k, n).astype(np.float32)
    by_word = np.ascontiguousarray(scaled.reshape(k // 512, 128, 4, n).transpose(0, 1, 3, 2))
    if fmt == "e4m3":
        words = by_word.astype(ml_dtypes.float8_e4m3fn).view(np.uint8)
    else:
        c = by_word.astype(ml_dtypes.float4_e2m1fn).view(np.uint8) & 0xF
        words = c[..., 0::2] | (c[..., 1::2] << 4)
    return np.ascontiguousarray(words), np.ascontiguousarray(byte.astype(np.uint8).reshape(k // 512, 16, n))


def unpack_weight(words, scales, fmt):
    g, p, n, _ = words.shape
    if fmt == "e4m3":
        vals = np.ascontiguousarray(words).view(ml_dtypes.float8_e4m3fn).astype(np.float64)
    else:
        nib = np.empty((g, p, n, 4), np.uint8)
        nib[..., 0::2] = words & 0xF
        nib[..., 1::2] = words >> 4
        vals = E2M1[nib]
    vals = vals * np.repeat(np.exp2(scales.astype(np.float64) - 127.0), 8, axis=1)[..., None]
    return vals.transpose(0, 1, 3, 2).reshape(g * 512, n)


B, I, HS, G = 128, 2048, 512, 3
H = HS * G
MXK = 16 * 32
HH_MX = H % MXK == 0


def sigmoid(v):
    return 1.0 / (1.0 + np.exp(-v))


def setup_inputs():
    s = mx_kscale(I)
    t = mx_kscale(H) if HH_MX else np.ones(H)
    inp = bf(np.random.standard_normal((B, I)) * s)
    h0 = bf(np.random.standard_normal((B, H)) * t)
    c0 = bf(np.random.standard_normal((B, H)))
    ih_words, ih_scales = pack_weight(np.random.standard_normal((I, 4 * H)) * 0.7 / np.sqrt(I) / s[:, None], "e4m3")
    hh_words, hh_scales = pack_weight(np.random.standard_normal((H, 4 * H)) * 0.7 / np.sqrt(H) / t[:, None], "e4m3")
    return {"input": inp,
            "h0": h0,
            "c0": c0,
            "weight_ih_words": ih_words,
            "weight_ih_scales": ih_scales,
            "weight_hh_words": hh_words,
            "weight_hh_scales": hh_scales,
            "bias_ih": bf(np.random.standard_normal(4 * H) * 0.3),
            "bias_hh": bf(np.random.standard_normal(4 * H) * 0.3)}


def reference(input, h0, c0, weight_ih_words, weight_ih_scales, weight_hh_words, weight_hh_scales, bias_ih, bias_hh):
    pi = mxq(f64(input), 1, "e4m3") @ unpack_weight(weight_ih_words, weight_ih_scales, "e4m3")
    if HH_MX:
        ph = mxq(f64(h0), 1, "e4m3") @ unpack_weight(weight_hh_words, weight_hh_scales, "e4m3")
    else:
        ph = f64(h0) @ unpack_weight(weight_hh_words, weight_hh_scales, "e4m3")
    gates = pi + f64(bias_ih) + ph + f64(bias_hh)
    c_in = f64(c0)
    h_parts, c_parts = [], []
    st = 0
    for _ in range(G):
        blk = gates[:, st * 4: st * 4 + 4 * HS]
        g, i, f, o = np.split(blk, 4, axis=-1)
        c1 = np.tanh(g) * sigmoid(i) + c_in[:, st: st + HS] * sigmoid(f)
        h_parts.append(np.tanh(c1) * sigmoid(o))
        c_parts.append(c1)
        st += HS
    return np.concatenate(h_parts, axis=-1), np.concatenate(c_parts, axis=-1)

@@ -1,0 +1,225 @@
+from contextlib import ExitStack
+
+import concourse.mybir as mybir
+from concourse.masks import make_identity
+
+F32 = mybir.dt.float32
+BF16 = mybir.dt.bfloat16
+I32 = mybir.dt.int32
+U32 = mybir.dt.uint32
+U8 = mybir.dt.uint8
+FP8X4 = mybir.dt.float8_e4m3fn_x4
+ACT = mybir.ActivationFunctionType
+ALU = mybir.AluOpType
+
+P = 128
+K_IH = 2048
+K_HH = 1536
+HS = 512
+GROUPS = 3
+H = HS * GROUPS
+NCOL = 4 * H
+PASS_IH = K_IH // 512
+PASS_HH = K_HH // 512
+PASSES = PASS_IH + PASS_HH
+W_BUFS = 12
+FLOPS = 2 * P * (K_IH + K_HH) * NCOL
+
+
+def tile_symlstmcell_w_kernel(
+    tc, x, h0, c0, ih_words, ih_scales, hh_words, hh_scales, bias_ih, bias_hh, out_h, out_c
+):
+    nc = tc.nc
+    with ExitStack() as ctx:
+        ctx.enter_context(tc.manual_schedule())
+        const = ctx.enter_context(tc.tile_pool(name="const", bufs=1))
+        wpool = ctx.enter_context(tc.tile_pool(name="wpool", bufs=W_BUFS))
+        work = ctx.enter_context(tc.tile_pool(name="work", bufs=2))
+        psum = ctx.enter_context(tc.psum_pool(name="psum", bufs=8))
+
+        x_sb = const.tile([P, K_IH], BF16)
+        h_sb = const.tile([P, K_HH], BF16)
+        c_sb = const.tile([P, H], BF16)
+        ident = const.tile([P, P], F32)
+        pick = const.tile([P, 4], BF16)
+        brow = const.tile([P, NCOL // 4], BF16)
+        warm = const.tile([P, 1], F32)
+        bias_sb = const.tile([P, NCOL], F32)
+        pl_ih = const.tile([P, NCOL], U8, align_bytes=64)
+        pl_hh = const.tile([P, NCOL], U8, align_bytes=64)
+        grp = const.tile([P, PASSES * 512], BF16, align_bytes=64)
+        xq = const.tile([P, PASSES * P], U32, align_bytes=64)
+        xs = const.tile([P, PASSES * P], U8, align_bytes=64)
+        c1_sb = const.tile([P, H], F32)
+        h1_sb = const.tile([P, H], F32)
+
+        nc.vector.memset(brow[:].bitcast(I32), 0)
+        nc.vector.memset(warm[:], 0.0)
+        nc.vector.memset(pl_ih[:].bitcast(I32), 0)
+        nc.vector.memset(pl_hh[:].bitcast(I32), 0)
+        make_identity(nc, ident[:])
+
+        nc.sync.dma_start(out=x_sb[:], in_=x)
+        nc.sync.dma_start(out=h_sb[:], in_=h0)
+        nc.scalar.dma_start(out=brow[0:4, :], in_=bias_ih.rearrange("(r c) -> r c", r=4))
+        nc.scalar.dma_start(out=brow[4:8, :], in_=bias_hh.rearrange("(r c) -> r c", r=4))
+        nc.scalar.dma_start(out=c_sb[:], in_=c0)
+        nc.scalar.activation(out=warm[:], in_=warm[:], func=ACT.Sigmoid)
+
+        ih_s32 = ih_scales.bitcast(I32)
+        hh_s32 = hh_scales.bitcast(I32)
+        for q in range(4):
+            nc.sync.dma_start(
+                out=pl_ih[32 * q : 32 * q + 4 * PASS_IH, :].bitcast(I32),
+                in_=ih_s32[:, 4 * q : 4 * q + 4, :],
+            )
+        for q in range(4):
+            nc.sync.dma_start(
+                out=pl_hh[32 * q : 32 * q + 4 * PASS_HH, :].bitcast(I32),
+                in_=hh_s32[:, 4 * q : 4 * q + 4, :],
+            )
+
+        chunks = [(j, g) for j in range(GROUPS) for g in range(PASSES)]
+        w_tiles = {}
+
+        def load_chunk(idx):
+            j, g = chunks[idx]
+            src = ih_words[g] if g < PASS_IH else hh_words[g - PASS_IH]
+            src = src.rearrange("p n t -> p (n t)")[:, 16 * HS * j : 16 * HS * (j + 1)]
+            wt = wpool.tile([P, 4 * HS], U32, align_bytes=64, name="wt", tag="wt")
+            nc.sync.dma_start(out=wt[:].bitcast(I32), in_=src.bitcast(I32))
+            w_tiles[idx] = wt
+
+        ahead = W_BUFS - 1
+        for idx in range(ahead):
+            load_chunk(idx)
+
+        nc.vector.tensor_tensor(out=pick[:], in0=ident[:, 0:4], in1=ident[:, 4:8], op=ALU.add)
+
+        xw = x_sb[:].bitcast(F32)
+        hw = h_sb[:].bitcast(F32)
+        grpw = grp[:].bitcast(F32)
+        banks = [(0, 2), (2, 2), (4, 2), (6, 1)]
+        t_tiles = []
+        for g0, ng in banks:
+            tt = psum.tile([P, 512], F32, name="tt", tag="bank")
+            for gl in range(ng):
+                g = g0 + gl
+                src = xw if g < PASS_IH else hw
+                gg = g if g < PASS_IH else g - PASS_IH
+                for u in range(2):
+                    nc.tensor.transpose(
+                        out=tt[:, 128 * (2 * gl + u) : 128 * (2 * gl + u + 1)],
+                        in_=src[:, 256 * gg + u : 256 * (gg + 1) : 2],
+                        identity=ident[:],
+                    )
+            t_tiles.append(tt)
+        for b, (g0, ng) in enumerate(banks):
+            dst = grpw[:, 256 * g0 : 256 * (g0 + ng)].rearrange(
+                "p (a m u) -> p a m u", a=ng, m=P, u=2
+            )
+            srcv = t_tiles[b][:, 0 : 256 * ng].rearrange("p (a u m) -> p a m u", a=ng, u=2, m=P)
+            if b % 2 == 0:
+                nc.vector.tensor_copy(out=dst, in_=srcv)
+            else:
+                nc.scalar.copy(out=dst, in_=srcv)
+        for g0, ng in banks:
+            nc.vector.quantize_mx(
+                out=xq[:, P * g0 : P * (g0 + ng)].bitcast(FP8X4),
+                scales=xs[:, P * g0 : P * (g0 + ng)],
+                in_=grp[:, 512 * g0 : 512 * (g0 + ng)],
+            )
+
+        for n in range(NCOL // 512):
+            bb = psum.tile([P, 512], F32, name="bb", tag="bank")
+            r, c = divmod(n, 3)
+            nc.tensor.matmul(
+                out=bb[:],
+                lhsT=pick[:, r : r + 1].to_broadcast([P, P]),
+                rhs=brow[:, 512 * c : 512 * (c + 1)],
+                start=True,
+                stop=True,
+            )
+            if n % 2 == 0:
+                nc.scalar.copy(out=bias_sb[:, 512 * n : 512 * (n + 1)], in_=bb[:])
+            else:
+                nc.vector.tensor_copy(out=bias_sb[:, 512 * n : 512 * (n + 1)], in_=bb[:])
+
+        gate_order = [1, 0, 2, 3]
+        half = HS // 2
+        for j in range(GROUPS):
+            acc = {}
+            for q in gate_order:
+                acc[q] = psum.tile([P, 512], F32, name="acc", tag="bank")
+            for g in range(PASSES):
+                idx = j * PASSES + g
+                if idx + ahead < len(chunks):
+                    load_chunk(idx + ahead)
+                wt = w_tiles[idx]
+                plane = pl_ih if g < PASS_IH else pl_hh
+                k = 4 * (g if g < PASS_IH else g - PASS_IH)
+                for q in gate_order:
+                    col = 4 * HS * j + HS * q
+                    nc.tensor.matmul_mx(
+                        out=acc[q][:],
+                        lhsT=xq[:, P * g : P * (g + 1)].bitcast(FP8X4),
+                        lhsT_scale=xs[:, P * g : P * (g + 1)],
+                        rhs=wt[:, HS * q : HS * (q + 1)].bitcast(FP8X4),
+                        rhs_scale=plane[k:P, col : col + HS],
+                        start=(g == 0),
+                        stop=(g == PASSES - 1),
+                    )
+            gt = work.tile([P, 4 * HS], F32, name="gt", tag="gt")
+            th = work.tile([P, HS], F32, name="th", tag="th")
+            for q in gate_order:
+                col = 4 * HS * j + HS * q
+                nc.vector.tensor_tensor(
+                    out=gt[:, HS * q : HS * (q + 1)],
+                    in0=acc[q][:],
+                    in1=bias_sb[:, col : col + HS],
+                    op=ALU.add,
+                )
+                nc.scalar.activation(
+                    out=gt[:, HS * q : HS * (q + 1)],
+                    in_=gt[:, HS * q : HS * (q + 1)],
+                    func=(ACT.Tanh if q == 0 else ACT.Sigmoid),
+                )
+            nc.vector.tensor_tensor(
+                out=gt[:, 0:HS], in0=gt[:, 0:HS], in1=gt[:, HS : 2 * HS], op=ALU.mult
+            )
+            nc.vector.tensor_tensor(
+                out=gt[:, 2 * HS : 3 * HS],
+                in0=c_sb[:, HS * j : HS * (j + 1)],
+                in1=gt[:, 2 * HS : 3 * HS],
+                op=ALU.mult,
+            )
+            for s in range(2):
+                lo = half * s
+                nc.vector.tensor_tensor(
+                    out=c1_sb[:, HS * j + lo : HS * j + lo + half],
+                    in0=gt[:, lo : lo + half],
+                    in1=gt[:, 2 * HS + lo : 2 * HS + lo + half],
+                    op=ALU.add,
+                )
+                nc.scalar.activation(
+                    out=th[:, lo : lo + half],
+                    in_=c1_sb[:, HS * j + lo : HS * j + lo + half],
+                    func=ACT.Tanh,
+                )
+            for s in range(2):
+                lo = half * s
+                nc.vector.tensor_tensor(
+                    out=h1_sb[:, HS * j + lo : HS * j + lo + half],
+                    in0=th[:, lo : lo + half],
+                    in1=gt[:, 3 * HS + lo : 3 * HS + lo + half],
+                    op=ALU.mult,
+                )
+            if j == 1:
+                nc.sync.dma_start(out=out_c[:, 0 : 2 * HS], in_=c1_sb[:, 0 : 2 * HS])
+                nc.sync.dma_start(out=out_h[:, 0 : 2 * HS], in_=h1_sb[:, 0 : 2 * HS])
+            if j == 2:
+                nc.sync.dma_start(out=out_c[:, 2 * HS : H], in_=c1_sb[:, 2 * HS : H])
+                nc.sync.dma_start(
+                    out=out_h[:, 2 * HS : 2 * HS + half], in_=h1_sb[:, 2 * HS : 2 * HS + half]
+                )
+                nc.sync.dma_start(out=out_h[:, 2 * HS + half : H], in_=h1_sb[:, 2 * HS + half : H])

@@ -53,31 +53,42 @@ def tile_symlstmcell_w_kernel(
         c1_sb = const.tile([P, H], F32)
         h1_sb = const.tile([P, H], F32)
 
-        nc.vector.memset(brow[:].bitcast(I32), 0)
-        nc.vector.memset(warm[:], 0.0)
         nc.vector.memset(pl_ih[:].bitcast(I32), 0)
         nc.vector.memset(pl_hh[:].bitcast(I32), 0)
+        nc.vector.memset(brow[:].bitcast(I32), 0)
+        nc.vector.memset(warm[:], 0.0)
         make_identity(nc, ident[:])
 
         nc.sync.dma_start(out=x_sb[:], in_=x)
-        nc.sync.dma_start(out=h_sb[:], in_=h0)
-        nc.scalar.dma_start(out=brow[0:4, :], in_=bias_ih.rearrange("(r c) -> r c", r=4))
-        nc.scalar.dma_start(out=brow[4:8, :], in_=bias_hh.rearrange("(r c) -> r c", r=4))
-        nc.scalar.dma_start(out=c_sb[:], in_=c0)
-        nc.scalar.activation(out=warm[:], in_=warm[:], func=ACT.Sigmoid)
+        nc.scalar.dma_start(out=h_sb[:], in_=h0)
 
         ih_s32 = ih_scales.bitcast(I32)
         hh_s32 = hh_scales.bitcast(I32)
-        for q in range(4):
+        ih_sf = ih_scales.bitcast(F32)
+        hh_sf = hh_scales.bitcast(F32)
+        for q in range(2):
             nc.sync.dma_start(
                 out=pl_ih[32 * q : 32 * q + 4 * PASS_IH, :].bitcast(I32),
                 in_=ih_s32[:, 4 * q : 4 * q + 4, :],
             )
-        for q in range(4):
+            nc.scalar.dma_start(
+                out=pl_ih[32 * q + 64 : 32 * q + 64 + 4 * PASS_IH, :].bitcast(F32),
+                in_=ih_sf[:, 4 * q + 8 : 4 * q + 12, :],
+            )
+        for q in range(2):
             nc.sync.dma_start(
                 out=pl_hh[32 * q : 32 * q + 4 * PASS_HH, :].bitcast(I32),
                 in_=hh_s32[:, 4 * q : 4 * q + 4, :],
             )
+            nc.scalar.dma_start(
+                out=pl_hh[32 * q + 64 : 32 * q + 64 + 4 * PASS_HH, :].bitcast(F32),
+                in_=hh_sf[:, 4 * q + 8 : 4 * q + 12, :],
+            )
+
+        nc.scalar.dma_start(out=brow[0:4, :], in_=bias_ih.rearrange("(r c) -> r c", r=4))
+        nc.scalar.dma_start(out=brow[4:8, :], in_=bias_hh.rearrange("(r c) -> r c", r=4))
+        nc.scalar.dma_start(out=c_sb[:], in_=c0)
+        nc.scalar.activation(out=warm[:], in_=warm[:], func=ACT.Sigmoid)
 
         chunks = [(j, g) for j in range(GROUPS) for g in range(PASSES)]
         w_tiles = {}

@@ -60,50 +60,55 @@ def tile_symlstmcell_w_kernel(
         make_identity(nc, ident[:])
 
         nc.sync.dma_start(out=x_sb[:], in_=x)
-        nc.scalar.dma_start(out=h_sb[:], in_=h0)
-
-        ih_s32 = ih_scales.bitcast(I32)
-        hh_s32 = hh_scales.bitcast(I32)
-        ih_sf = ih_scales.bitcast(F32)
-        hh_sf = hh_scales.bitcast(F32)
-        for q in range(2):
-            nc.sync.dma_start(
-                out=pl_ih[32 * q : 32 * q + 4 * PASS_IH, :].bitcast(I32),
-                in_=ih_s32[:, 4 * q : 4 * q + 4, :],
-            )
-            nc.scalar.dma_start(
-                out=pl_ih[32 * q + 64 : 32 * q + 64 + 4 * PASS_IH, :].bitcast(F32),
-                in_=ih_sf[:, 4 * q + 8 : 4 * q + 12, :],
-            )
-        for q in range(2):
-            nc.sync.dma_start(
-                out=pl_hh[32 * q : 32 * q + 4 * PASS_HH, :].bitcast(I32),
-                in_=hh_s32[:, 4 * q : 4 * q + 4, :],
-            )
-            nc.scalar.dma_start(
-                out=pl_hh[32 * q + 64 : 32 * q + 64 + 4 * PASS_HH, :].bitcast(F32),
-                in_=hh_sf[:, 4 * q + 8 : 4 * q + 12, :],
-            )
-
+        nc.sync.dma_start(out=h_sb[:], in_=h0)
         nc.scalar.dma_start(out=brow[0:4, :], in_=bias_ih.rearrange("(r c) -> r c", r=4))
         nc.scalar.dma_start(out=brow[4:8, :], in_=bias_hh.rearrange("(r c) -> r c", r=4))
         nc.scalar.dma_start(out=c_sb[:], in_=c0)
         nc.scalar.activation(out=warm[:], in_=warm[:], func=ACT.Sigmoid)
 
-        chunks = [(j, g) for j in range(GROUPS) for g in range(PASSES)]
-        w_tiles = {}
+        ih_s32 = ih_scales.bitcast(I32)
+        hh_s32 = hh_scales.bitcast(I32)
+        for q in range(4):
+            nc.sync.dma_start(
+                out=pl_ih[32 * q : 32 * q + 4 * PASS_IH, :].bitcast(I32),
+                in_=ih_s32[:, 4 * q : 4 * q + 4, :],
+            )
+        for q in range(4):
+            nc.sync.dma_start(
+                out=pl_hh[32 * q : 32 * q + 4 * PASS_HH, :].bitcast(I32),
+                in_=hh_s32[:, 4 * q : 4 * q + 4, :],
+            )
 
-        def load_chunk(idx):
-            j, g = chunks[idx]
-            src = ih_words[g] if g < PASS_IH else hh_words[g - PASS_IH]
-            src = src.rearrange("p n t -> p (n t)")[:, 16 * HS * j : 16 * HS * (j + 1)]
+        last = GROUPS - 1
+        loads = [(g, 1, 4 * HS * j, 4 * HS) for j in range(last) for g in range(PASSES)]
+        loads += [(g, 1, 4 * HS * last, 3 * HS) for g in range(PASSES)]
+        loads += [(0, 4, 4 * HS * last + 3 * HS, HS), (4, 2, 4 * HS * last + 3 * HS, HS)]
+        loads += [(6, 1, 4 * HS * last + 3 * HS, HS)]
+        rhs_of = {}
+
+        def load_weights(idx):
+            g0, ng, col0, ncol = loads[idx]
+            words = ih_words if g0 < PASS_IH else hh_words
+            gg = g0 if g0 < PASS_IH else g0 - PASS_IH
+            src = words[gg : gg + ng, :, col0 : col0 + ncol, :].rearrange("g p n t -> p g (n t)")
             wt = wpool.tile([P, 4 * HS], U32, align_bytes=64, name="wt", tag="wt")
-            nc.sync.dma_start(out=wt[:].bitcast(I32), in_=src.bitcast(I32))
-            w_tiles[idx] = wt
+            nc.sync.dma_start(
+                out=wt[:, 0 : ng * ncol].bitcast(I32).rearrange("p (g n) -> p g n", g=ng),
+                in_=src.bitcast(I32),
+            )
+            for a in range(ng):
+                for c in range(ncol // HS):
+                    rhs_of[(g0 + a, col0 // HS + c)] = wt[:, a * ncol + c * HS : a * ncol + (c + 1) * HS]
 
         ahead = W_BUFS - 1
         for idx in range(ahead):
-            load_chunk(idx)
+            load_weights(idx)
+        issued = [ahead]
+
+        def next_load():
+            if issued[0] < len(loads):
+                load_weights(issued[0])
+                issued[0] = issued[0] + 1
 
         nc.vector.tensor_tensor(out=pick[:], in0=ident[:, 0:4], in1=ident[:, 4:8], op=ALU.add)
 
@@ -156,45 +161,48 @@ def tile_symlstmcell_w_kernel(
             else:
                 nc.vector.tensor_copy(out=bias_sb[:, 512 * n : 512 * (n + 1)], in_=bb[:])
 
-        gate_order = [1, 0, 2, 3]
         half = HS // 2
+
+        def mx_pass(acc_tile, g, n):
+            plane = pl_ih if g < PASS_IH else pl_hh
+            k = 4 * (g if g < PASS_IH else g - PASS_IH)
+            nc.tensor.matmul_mx(
+                out=acc_tile[:],
+                lhsT=xq[:, P * g : P * (g + 1)].bitcast(FP8X4),
+                lhsT_scale=xs[:, P * g : P * (g + 1)],
+                rhs=rhs_of[(g, n)].bitcast(FP8X4),
+                rhs_scale=plane[k:P, HS * n : HS * (n + 1)],
+                start=(g == 0),
+                stop=(g == PASSES - 1),
+            )
+
+        def gate(gt, acc_tile, j, q, lo, width):
+            col = 4 * HS * j + HS * q + lo
+            nc.vector.tensor_tensor(
+                out=gt[:, HS * q + lo : HS * q + lo + width],
+                in0=acc_tile[:, lo : lo + width],
+                in1=bias_sb[:, col : col + width],
+                op=ALU.add,
+            )
+            nc.scalar.activation(
+                out=gt[:, HS * q + lo : HS * q + lo + width],
+                in_=gt[:, HS * q + lo : HS * q + lo + width],
+                func=(ACT.Tanh if q == 0 else ACT.Sigmoid),
+            )
+
         for j in range(GROUPS):
             acc = {}
-            for q in gate_order:
+            for q in (1, 0, 2, 3):
                 acc[q] = psum.tile([P, 512], F32, name="acc", tag="bank")
-            for g in range(PASSES):
-                idx = j * PASSES + g
-                if idx + ahead < len(chunks):
-                    load_chunk(idx + ahead)
-                wt = w_tiles[idx]
-                plane = pl_ih if g < PASS_IH else pl_hh
-                k = 4 * (g if g < PASS_IH else g - PASS_IH)
-                for q in gate_order:
-                    col = 4 * HS * j + HS * q
-                    nc.tensor.matmul_mx(
-                        out=acc[q][:],
-                        lhsT=xq[:, P * g : P * (g + 1)].bitcast(FP8X4),
-                        lhsT_scale=xs[:, P * g : P * (g + 1)],
-                        rhs=wt[:, HS * q : HS * (q + 1)].bitcast(FP8X4),
-                        rhs_scale=plane[k:P, col : col + HS],
-                        start=(g == 0),
-                        stop=(g == PASSES - 1),
-                    )
             gt = work.tile([P, 4 * HS], F32, name="gt", tag="gt")
             th = work.tile([P, HS], F32, name="th", tag="th")
-            for q in gate_order:
-                col = 4 * HS * j + HS * q
-                nc.vector.tensor_tensor(
-                    out=gt[:, HS * q : HS * (q + 1)],
-                    in0=acc[q][:],
-                    in1=bias_sb[:, col : col + HS],
-                    op=ALU.add,
-                )
-                nc.scalar.activation(
-                    out=gt[:, HS * q : HS * (q + 1)],
-                    in_=gt[:, HS * q : HS * (q + 1)],
-                    func=(ACT.Tanh if q == 0 else ACT.Sigmoid),
-                )
+            early = (1, 0, 2, 3) if j < last else (1, 0, 2)
+            for g in range(PASSES):
+                next_load()
+                for q in early:
+                    mx_pass(acc[q], g, 4 * j + q)
+            for q in early:
+                gate(gt, acc[q], j, q, 0, HS)
             nc.vector.tensor_tensor(
                 out=gt[:, 0:HS], in0=gt[:, 0:HS], in1=gt[:, HS : 2 * HS], op=ALU.mult
             )
@@ -217,6 +225,11 @@ def tile_symlstmcell_w_kernel(
                     in_=c1_sb[:, HS * j + lo : HS * j + lo + half],
                     func=ACT.Tanh,
                 )
+            if j == last:
+                for g in range(PASSES):
+                    mx_pass(acc[3], g, 4 * j + 3)
+                for s in range(2):
+                    gate(gt, acc[3], j, 3, half * s, half)
             for s in range(2):
                 lo = half * s
                 nc.vector.tensor_tensor(
@@ -225,12 +238,15 @@ def tile_symlstmcell_w_kernel(
                     in1=gt[:, 3 * HS + lo : 3 * HS + lo + half],
                     op=ALU.mult,
                 )
-            if j == 1:
-                nc.sync.dma_start(out=out_c[:, 0 : 2 * HS], in_=c1_sb[:, 0 : 2 * HS])
-                nc.sync.dma_start(out=out_h[:, 0 : 2 * HS], in_=h1_sb[:, 0 : 2 * HS])
-            if j == 2:
-                nc.sync.dma_start(out=out_c[:, 2 * HS : H], in_=c1_sb[:, 2 * HS : H])
-                nc.sync.dma_start(
-                    out=out_h[:, 2 * HS : 2 * HS + half], in_=h1_sb[:, 2 * HS : 2 * HS + half]
-                )
-                nc.sync.dma_start(out=out_h[:, 2 * HS + half : H], in_=h1_sb[:, 2 * HS + half : H])
+            cols = slice(HS * j, HS * (j + 1))
+            if j == 0:
+                nc.scalar.dma_start(out=out_c[:, cols], in_=c1_sb[:, cols])
+                nc.scalar.dma_start(out=out_h[:, cols], in_=h1_sb[:, cols])
+            elif j < last:
+                nc.sync.dma_start(out=out_c[:, cols], in_=c1_sb[:, cols])
+                nc.sync.dma_start(out=out_h[:, cols], in_=h1_sb[:, cols])
+            else:
+                nc.sync.dma_start(out=out_c[:, cols], in_=c1_sb[:, cols])
+                for s in range(2):
+                    lo = HS * j + half * s
+                    nc.sync.dma_start(out=out_h[:, lo : lo + half], in_=h1_sb[:, lo : lo + half])

@@ -22,7 +22,7 @@ NCOL = 4 * H
 PASS_IH = K_IH // 512
 PASS_HH = K_HH // 512
 PASSES = PASS_IH + PASS_HH
-W_BUFS = 12
+W_BUFS = 7
 FLOPS = 2 * P * (K_IH + K_HH) * NCOL
 
 
@@ -80,7 +80,7 @@ def tile_symlstmcell_w_kernel(
             )
 
         last = GROUPS - 1
-        loads = [(g, 1, 4 * HS * j, 4 * HS) for j in range(last) for g in range(PASSES)]
+        loads = [(g, 1, 0, 4 * HS * last) for g in range(PASSES)]
         loads += [(g, 1, 4 * HS * last, 3 * HS) for g in range(PASSES)]
         loads += [(0, 4, 4 * HS * last + 3 * HS, HS), (4, 2, 4 * HS * last + 3 * HS, HS)]
         loads += [(6, 1, 4 * HS * last + 3 * HS, HS)]
@@ -91,7 +91,7 @@ def tile_symlstmcell_w_kernel(
             words = ih_words if g0 < PASS_IH else hh_words
             gg = g0 if g0 < PASS_IH else g0 - PASS_IH
             src = words[gg : gg + ng, :, col0 : col0 + ncol, :].rearrange("g p n t -> p g (n t)")
-            wt = wpool.tile([P, 4 * HS], U32, align_bytes=64, name="wt", tag="wt")
+            wt = wpool.tile([P, 4 * HS * last], U32, align_bytes=64, name="wt", tag="wt")
             nc.sync.dma_start(
                 out=wt[:, 0 : ng * ncol].bitcast(I32).rearrange("p (g n) -> p g n", g=ng),
                 in_=src.bitcast(I32),
@@ -190,19 +190,7 @@ def tile_symlstmcell_w_kernel(
                 func=(ACT.Tanh if q == 0 else ACT.Sigmoid),
             )
 
-        for j in range(GROUPS):
-            acc = {}
-            for q in (1, 0, 2, 3):
-                acc[q] = psum.tile([P, 512], F32, name="acc", tag="bank")
-            gt = work.tile([P, 4 * HS], F32, name="gt", tag="gt")
-            th = work.tile([P, HS], F32, name="th", tag="th")
-            early = (1, 0, 2, 3) if j < last else (1, 0, 2)
-            for g in range(PASSES):
-                next_load()
-                for q in early:
-                    mx_pass(acc[q], g, 4 * j + q)
-            for q in early:
-                gate(gt, acc[q], j, q, 0, HS)
+        def cell(gt, th, j):
             nc.vector.tensor_tensor(
                 out=gt[:, 0:HS], in0=gt[:, 0:HS], in1=gt[:, HS : 2 * HS], op=ALU.mult
             )
@@ -225,11 +213,8 @@ def tile_symlstmcell_w_kernel(
                     in_=c1_sb[:, HS * j + lo : HS * j + lo + half],
                     func=ACT.Tanh,
                 )
-            if j == last:
-                for g in range(PASSES):
-                    mx_pass(acc[3], g, 4 * j + 3)
-                for s in range(2):
-                    gate(gt, acc[3], j, 3, half * s, half)
+
+        def hidden(gt, th, j):
             for s in range(2):
                 lo = half * s
                 nc.vector.tensor_tensor(
@@ -238,15 +223,50 @@ def tile_symlstmcell_w_kernel(
                     in1=gt[:, 3 * HS + lo : 3 * HS + lo + half],
                     op=ALU.mult,
                 )
-            cols = slice(HS * j, HS * (j + 1))
+
+        order = (1, 0, 2, 3)
+        acc = {}
+
+        for j in range(last):
+            for q in order:
+                acc[(j, q)] = psum.tile([P, 512], F32, name="acc", tag="bank")
+        for g in range(PASSES):
+            next_load()
+            for j in range(last):
+                for q in order:
+                    mx_pass(acc[(j, q)], g, 4 * j + q)
+        for j in range(last):
+            gt = work.tile([P, 4 * HS], F32, name="gt", tag="gt")
+            th = work.tile([P, HS], F32, name="th", tag="th")
+            for q in order:
+                gate(gt, acc[(j, q)], j, q, 0, HS)
+            cell(gt, th, j)
             if j == 0:
-                nc.scalar.dma_start(out=out_c[:, cols], in_=c1_sb[:, cols])
-                nc.scalar.dma_start(out=out_h[:, cols], in_=h1_sb[:, cols])
-            elif j < last:
-                nc.sync.dma_start(out=out_c[:, cols], in_=c1_sb[:, cols])
-                nc.sync.dma_start(out=out_h[:, cols], in_=h1_sb[:, cols])
-            else:
-                nc.sync.dma_start(out=out_c[:, cols], in_=c1_sb[:, cols])
-                for s in range(2):
-                    lo = HS * j + half * s
-                    nc.sync.dma_start(out=out_h[:, lo : lo + half], in_=h1_sb[:, lo : lo + half])
+                nc.scalar.dma_start(out=out_c[:, 0:HS], in_=c1_sb[:, 0:HS])
+            hidden(gt, th, j)
+
+        j = last
+        for q in order:
+            acc[(j, q)] = psum.tile([P, 512], F32, name="acc", tag="bank")
+        gt = work.tile([P, 4 * HS], F32, name="gt", tag="gt")
+        th = work.tile([P, HS], F32, name="th", tag="th")
+        for g in range(PASSES):
+            next_load()
+            for q in order[0:3]:
+                mx_pass(acc[(j, q)], g, 4 * j + q)
+        for q in order[0:3]:
+            gate(gt, acc[(j, q)], j, q, 0, HS)
+        cell(gt, th, j)
+        for g in range(PASSES):
+            mx_pass(acc[(j, 3)], g, 4 * j + 3)
+        for s in range(2):
+            gate(gt, acc[(j, 3)], j, 3, half * s, half)
+        hidden(gt, th, j)
+
+        nc.sync.dma_start(out=out_h[:, 0:HS], in_=h1_sb[:, 0:HS])
+        nc.sync.dma_start(out=out_c[:, HS : 2 * HS], in_=c1_sb[:, HS : 2 * HS])
+        nc.sync.dma_start(out=out_h[:, HS : 2 * HS], in_=h1_sb[:, HS : 2 * HS])
+        nc.sync.dma_start(out=out_c[:, 2 * HS : H], in_=c1_sb[:, 2 * HS : H])
+        for s in range(2):
+            lo = HS * j + half * s
+            nc.sync.dma_start(out=out_h[:, lo : lo + half], in_=h1_sb[:, lo : lo + half])

@@ -66,18 +66,20 @@ def tile_symlstmcell_w_kernel(
         nc.scalar.dma_start(out=c_sb[:], in_=c0)
         nc.scalar.activation(out=warm[:], in_=warm[:], func=ACT.Sigmoid)
 
-        ih_s32 = ih_scales.bitcast(I32)
-        hh_s32 = hh_scales.bitcast(I32)
+        ih_sf = ih_scales.bitcast(F32)
+        hh_sf = hh_scales.bitcast(F32)
         for q in range(4):
-            nc.sync.dma_start(
-                out=pl_ih[32 * q : 32 * q + 4 * PASS_IH, :].bitcast(I32),
-                in_=ih_s32[:, 4 * q : 4 * q + 4, :],
-            )
+            for r in range(4):
+                nc.gpsimd.dma_start(
+                    out=pl_ih[32 * q + r : 32 * q + 4 * PASS_IH : 4, :].bitcast(F32),
+                    in_=ih_sf[:, 4 * q + r, :],
+                )
         for q in range(4):
-            nc.sync.dma_start(
-                out=pl_hh[32 * q : 32 * q + 4 * PASS_HH, :].bitcast(I32),
-                in_=hh_s32[:, 4 * q : 4 * q + 4, :],
-            )
+            for r in range(4):
+                nc.gpsimd.dma_start(
+                    out=pl_hh[32 * q + r : 32 * q + 4 * PASS_HH : 4, :].bitcast(F32),
+                    in_=hh_sf[:, 4 * q + r, :],
+                )
 
         last = GROUPS - 1
         loads = [(g, 1, 0, 4 * HS * last) for g in range(PASSES)]

@@ -66,20 +66,18 @@ def tile_symlstmcell_w_kernel(
         nc.scalar.dma_start(out=c_sb[:], in_=c0)
         nc.scalar.activation(out=warm[:], in_=warm[:], func=ACT.Sigmoid)
 
-        ih_sf = ih_scales.bitcast(F32)
-        hh_sf = hh_scales.bitcast(F32)
+        ih_s32 = ih_scales.bitcast(I32)
+        hh_s32 = hh_scales.bitcast(I32)
         for q in range(4):
-            for r in range(4):
-                nc.gpsimd.dma_start(
-                    out=pl_ih[32 * q + r : 32 * q + 4 * PASS_IH : 4, :].bitcast(F32),
-                    in_=ih_sf[:, 4 * q + r, :],
-                )
+            nc.sync.dma_start(
+                out=pl_ih[32 * q : 32 * q + 4 * PASS_IH, :].bitcast(I32),
+                in_=ih_s32[:, 4 * q : 4 * q + 4, :],
+            )
         for q in range(4):
-            for r in range(4):
-                nc.gpsimd.dma_start(
-                    out=pl_hh[32 * q + r : 32 * q + 4 * PASS_HH : 4, :].bitcast(F32),
-                    in_=hh_sf[:, 4 * q + r, :],
-                )
+            nc.sync.dma_start(
+                out=pl_hh[32 * q : 32 * q + 4 * PASS_HH, :].bitcast(I32),
+                in_=hh_s32[:, 4 * q : 4 * q + 4, :],
+            )
 
         last = GROUPS - 1
         loads = [(g, 1, 0, 4 * HS * last) for g in range(PASSES)]
@@ -243,8 +241,6 @@ def tile_symlstmcell_w_kernel(
             for q in order:
                 gate(gt, acc[(j, q)], j, q, 0, HS)
             cell(gt, th, j)
-            if j == 0:
-                nc.scalar.dma_start(out=out_c[:, 0:HS], in_=c1_sb[:, 0:HS])
             hidden(gt, th, j)
 
         j = last
@@ -265,9 +261,8 @@ def tile_symlstmcell_w_kernel(
             gate(gt, acc[(j, 3)], j, 3, half * s, half)
         hidden(gt, th, j)
 
-        nc.sync.dma_start(out=out_h[:, 0:HS], in_=h1_sb[:, 0:HS])
-        nc.sync.dma_start(out=out_c[:, HS : 2 * HS], in_=c1_sb[:, HS : 2 * HS])
-        nc.sync.dma_start(out=out_h[:, HS : 2 * HS], in_=h1_sb[:, HS : 2 * HS])
+        nc.sync.dma_start(out=out_c[:, 0 : 2 * HS], in_=c1_sb[:, 0 : 2 * HS])
+        nc.sync.dma_start(out=out_h[:, 0 : 2 * HS], in_=h1_sb[:, 0 : 2 * HS])
         nc.sync.dma_start(out=out_c[:, 2 * HS : H], in_=c1_sb[:, 2 * HS : H])
         for s in range(2):
             lo = HS * j + half * s

@@ -53,31 +53,31 @@ def tile_symlstmcell_w_kernel(
         c1_sb = const.tile([P, H], F32)
         h1_sb = const.tile([P, H], F32)
 
+        nc.vector.memset(brow[:].bitcast(I32), 0)
         nc.vector.memset(pl_ih[:].bitcast(I32), 0)
         nc.vector.memset(pl_hh[:].bitcast(I32), 0)
-        nc.vector.memset(brow[:].bitcast(I32), 0)
         nc.vector.memset(warm[:], 0.0)
         make_identity(nc, ident[:])
 
         nc.sync.dma_start(out=x_sb[:], in_=x)
         nc.sync.dma_start(out=h_sb[:], in_=h0)
-        nc.scalar.dma_start(out=brow[0:4, :], in_=bias_ih.rearrange("(r c) -> r c", r=4))
-        nc.scalar.dma_start(out=brow[4:8, :], in_=bias_hh.rearrange("(r c) -> r c", r=4))
-        nc.scalar.dma_start(out=c_sb[:], in_=c0)
+        nc.sync.dma_start(out=brow[0:4, :], in_=bias_ih.rearrange("(r c) -> r c", r=4))
+        nc.sync.dma_start(out=brow[4:8, :], in_=bias_hh.rearrange("(r c) -> r c", r=4))
         nc.scalar.activation(out=warm[:], in_=warm[:], func=ACT.Sigmoid)
 
         ih_s32 = ih_scales.bitcast(I32)
         hh_s32 = hh_scales.bitcast(I32)
-        for q in range(4):
-            nc.sync.dma_start(
-                out=pl_ih[32 * q : 32 * q + 4 * PASS_IH, :].bitcast(I32),
-                in_=ih_s32[:, 4 * q : 4 * q + 4, :],
-            )
-        for q in range(4):
-            nc.sync.dma_start(
-                out=pl_hh[32 * q : 32 * q + 4 * PASS_HH, :].bitcast(I32),
-                in_=hh_s32[:, 4 * q : 4 * q + 4, :],
-            )
+        for pair in ((2, 3), (0, 1)):
+            for q in pair:
+                nc.sync.dma_start(
+                    out=pl_ih[32 * q : 32 * q + 4 * PASS_IH, :].bitcast(I32),
+                    in_=ih_s32[:, 4 * q : 4 * q + 4, :],
+                )
+            for q in pair:
+                nc.sync.dma_start(
+                    out=pl_hh[32 * q : 32 * q + 4 * PASS_HH, :].bitcast(I32),
+                    in_=hh_s32[:, 4 * q : 4 * q + 4, :],
+                )
 
         last = GROUPS - 1
         loads = [(g, 1, 0, 4 * HS * last) for g in range(PASSES)]
@@ -92,6 +92,13 @@ def tile_symlstmcell_w_kernel(
             gg = g0 if g0 < PASS_IH else g0 - PASS_IH
             src = words[gg : gg + ng, :, col0 : col0 + ncol, :].rearrange("g p n t -> p g (n t)")
             wt = wpool.tile([P, 4 * HS * last], U32, align_bytes=64, name="wt", tag="wt")
+            if idx == 0:
+                nc.vector.tensor_copy(
+                    out=wt[64:P, 0:1].bitcast(I32), in_=pl_ih[64:P, 0:4].bitcast(I32)
+                )
+                nc.vector.tensor_copy(
+                    out=wt[64:P, 1:2].bitcast(I32), in_=pl_hh[64:P, 0:4].bitcast(I32)
+                )
             nc.sync.dma_start(
                 out=wt[:, 0 : ng * ncol].bitcast(I32).rearrange("p (g n) -> p g n", g=ng),
                 in_=src.bitcast(I32),
@@ -103,6 +110,8 @@ def tile_symlstmcell_w_kernel(
         ahead = W_BUFS - 1
         for idx in range(ahead):
             load_weights(idx)
+            if idx == 0:
+                nc.sync.dma_start(out=c_sb[:], in_=c0)
         issued = [ahead]
 
         def next_load():

@@ -96,9 +96,6 @@ def tile_symlstmcell_w_kernel(
                 nc.vector.tensor_copy(
                     out=wt[64:P, 0:1].bitcast(I32), in_=pl_ih[64:P, 0:4].bitcast(I32)
                 )
-                nc.vector.tensor_copy(
-                    out=wt[64:P, 1:2].bitcast(I32), in_=pl_hh[64:P, 0:4].bitcast(I32)
-                )
             nc.sync.dma_start(
                 out=wt[:, 0 : ng * ncol].bitcast(I32).rearrange("p (g n) -> p g n", g=ng),
                 in_=src.bitcast(I32),

@@ -80,10 +80,11 @@ def tile_symlstmcell_w_kernel(
                 )
 
         last = GROUPS - 1
+        half = HS // 2
         loads = [(g, 1, 0, 4 * HS * last) for g in range(PASSES)]
         loads += [(g, 1, 4 * HS * last, 3 * HS) for g in range(PASSES)]
         loads += [(0, 4, 4 * HS * last + 3 * HS, HS), (4, 2, 4 * HS * last + 3 * HS, HS)]
-        loads += [(6, 1, 4 * HS * last + 3 * HS, HS)]
+        loads += [(6, 1, 4 * HS * last + 3 * HS + s * half, half) for s in range(2)]
         rhs_of = {}
 
         def load_weights(idx):
@@ -101,8 +102,8 @@ def tile_symlstmcell_w_kernel(
                 in_=src.bitcast(I32),
             )
             for a in range(ng):
-                for c in range(ncol // HS):
-                    rhs_of[(g0 + a, col0 // HS + c)] = wt[:, a * ncol + c * HS : a * ncol + (c + 1) * HS]
+                for c in range(ncol // half):
+                    rhs_of[(g0 + a, col0 // half + c)] = (wt, a * ncol + c * half)
 
         ahead = W_BUFS - 1
         for idx in range(ahead):
@@ -167,26 +168,25 @@ def tile_symlstmcell_w_kernel(
             else:
                 nc.vector.tensor_copy(out=bias_sb[:, 512 * n : 512 * (n + 1)], in_=bb[:])
 
-        half = HS // 2
-
-        def mx_pass(acc_tile, g, n):
+        def mx_pass(acc_tile, g, col, width):
+            wt, at = rhs_of[(g, col // half)]
             plane = pl_ih if g < PASS_IH else pl_hh
             k = 4 * (g if g < PASS_IH else g - PASS_IH)
             nc.tensor.matmul_mx(
-                out=acc_tile[:],
+                out=acc_tile[:, 0:width],
                 lhsT=xq[:, P * g : P * (g + 1)].bitcast(FP8X4),
                 lhsT_scale=xs[:, P * g : P * (g + 1)],
-                rhs=rhs_of[(g, n)].bitcast(FP8X4),
-                rhs_scale=plane[k:P, HS * n : HS * (n + 1)],
+                rhs=wt[:, at : at + width].bitcast(FP8X4),
+                rhs_scale=plane[k:P, col : col + width],
                 start=(g == 0),
                 stop=(g == PASSES - 1),
             )
 
-        def gate(gt, acc_tile, j, q, lo, width):
+        def gate(gt, sums, j, q, lo, width):
             col = 4 * HS * j + HS * q + lo
             nc.vector.tensor_tensor(
                 out=gt[:, HS * q + lo : HS * q + lo + width],
-                in0=acc_tile[:, lo : lo + width],
+                in0=sums,
                 in1=bias_sb[:, col : col + width],
                 op=ALU.add,
             )
@@ -220,15 +220,13 @@ def tile_symlstmcell_w_kernel(
                     func=ACT.Tanh,
                 )
 
-        def hidden(gt, th, j):
-            for s in range(2):
-                lo = half * s
-                nc.vector.tensor_tensor(
-                    out=h1_sb[:, HS * j + lo : HS * j + lo + half],
-                    in0=th[:, lo : lo + half],
-                    in1=gt[:, 3 * HS + lo : 3 * HS + lo + half],
-                    op=ALU.mult,
-                )
+        def hidden(gt, th, j, lo, width):
+            nc.vector.tensor_tensor(
+                out=h1_sb[:, HS * j + lo : HS * j + lo + width],
+                in0=th[:, lo : lo + width],
+                in1=gt[:, 3 * HS + lo : 3 * HS + lo + width],
+                op=ALU.mult,
+            )
 
         order = (1, 0, 2, 3)
         acc = {}
@@ -240,32 +238,39 @@ def tile_symlstmcell_w_kernel(
             next_load()
             for j in range(last):
                 for q in order:
-                    mx_pass(acc[(j, q)], g, 4 * j + q)
+                    mx_pass(acc[(j, q)], g, HS * (4 * j + q), HS)
         for j in range(last):
             gt = work.tile([P, 4 * HS], F32, name="gt", tag="gt")
             th = work.tile([P, HS], F32, name="th", tag="th")
             for q in order:
-                gate(gt, acc[(j, q)], j, q, 0, HS)
+                gate(gt, acc[(j, q)][:], j, q, 0, HS)
             cell(gt, th, j)
-            hidden(gt, th, j)
+            for s in range(2):
+                hidden(gt, th, j, half * s, half)
 
         j = last
-        for q in order:
+        for q in order[0:3]:
             acc[(j, q)] = psum.tile([P, 512], F32, name="acc", tag="bank")
         gt = work.tile([P, 4 * HS], F32, name="gt", tag="gt")
         th = work.tile([P, HS], F32, name="th", tag="th")
         for g in range(PASSES):
             next_load()
             for q in order[0:3]:
-                mx_pass(acc[(j, q)], g, 4 * j + q)
+                mx_pass(acc[(j, q)], g, HS * (4 * j + q), HS)
         for q in order[0:3]:
-            gate(gt, acc[(j, q)], j, q, 0, HS)
+            gate(gt, acc[(j, q)][:], j, q, 0, HS)
         cell(gt, th, j)
-        for g in range(PASSES):
-            mx_pass(acc[(j, 3)], g, 4 * j + 3)
+        o_acc = []
         for s in range(2):
-            gate(gt, acc[(j, 3)], j, 3, half * s, half)
-        hidden(gt, th, j)
+            oa = psum.tile([P, 512], F32, name="oa", tag="bank")
+            o_acc.append(oa)
+        for g in range(PASSES):
+            for s in range(2):
+                mx_pass(o_acc[s], g, HS * (4 * j + 3) + half * s, half)
+        for s in range(2):
+            gate(gt, o_acc[s][:, 0:half], j, 3, half * s, half)
+        for s in range(2):
+            hidden(gt, th, j, half * s, half)
 
         nc.sync.dma_start(out=out_c[:, 0 : 2 * HS], in_=c1_sb[:, 0 : 2 * HS])
         nc.sync.dma_start(out=out_h[:, 0 : 2 * HS], in_=h1_sb[:, 0 : 2 * HS])

@@ -23,6 +23,9 @@ PASS_IH = K_IH // 512
 PASS_HH = K_HH // 512
 PASSES = PASS_IH + PASS_HH
 W_BUFS = 7
+SLOT = NCOL // 4
+ROWS = 16
+PIECE = NCOL // ROWS
 FLOPS = 2 * P * (K_IH + K_HH) * NCOL
 
 
@@ -41,43 +44,50 @@ def tile_symlstmcell_w_kernel(
         h_sb = const.tile([P, K_HH], BF16)
         c_sb = const.tile([P, H], BF16)
         ident = const.tile([P, P], F32)
-        pick = const.tile([P, 4], BF16)
-        brow = const.tile([P, NCOL // 4], BF16)
+        pick = const.tile([P, ROWS], BF16)
+        brow = const.tile([P, PIECE], BF16)
         warm = const.tile([P, 1], F32)
         bias_sb = const.tile([P, NCOL], F32)
         pl_ih = const.tile([P, NCOL], U8, align_bytes=64)
-        pl_hh = const.tile([P, NCOL], U8, align_bytes=64)
+        pl_hh = const.tile([P, PASS_HH * SLOT], U8, align_bytes=64)
         grp = const.tile([P, PASSES * 512], BF16, align_bytes=64)
         xq = const.tile([P, PASSES * P], U32, align_bytes=64)
         xs = const.tile([P, PASSES * P], U8, align_bytes=64)
         c1_sb = const.tile([P, H], F32)
         h1_sb = const.tile([P, H], F32)
 
-        nc.vector.memset(brow[:].bitcast(I32), 0)
         nc.vector.memset(pl_ih[:].bitcast(I32), 0)
         nc.vector.memset(pl_hh[:].bitcast(I32), 0)
+        nc.vector.memset(brow[:].bitcast(I32), 0)
         nc.vector.memset(warm[:], 0.0)
         make_identity(nc, ident[:])
 
         nc.sync.dma_start(out=x_sb[:], in_=x)
         nc.sync.dma_start(out=h_sb[:], in_=h0)
-        nc.sync.dma_start(out=brow[0:4, :], in_=bias_ih.rearrange("(r c) -> r c", r=4))
-        nc.sync.dma_start(out=brow[4:8, :], in_=bias_hh.rearrange("(r c) -> r c", r=4))
         nc.scalar.activation(out=warm[:], in_=warm[:], func=ACT.Sigmoid)
 
         ih_s32 = ih_scales.bitcast(I32)
-        hh_s32 = hh_scales.bitcast(I32)
-        for pair in ((2, 3), (0, 1)):
-            for q in pair:
+        hh_s32 = hh_scales.rearrange("g q (s c) -> g s q c", s=4).bitcast(I32)
+
+        def load_ih_scales(q):
+            nc.sync.dma_start(
+                out=pl_ih[32 * q : 32 * q + 4 * PASS_IH, :].bitcast(I32),
+                in_=ih_s32[:, 4 * q : 4 * q + 4, :],
+            )
+
+        def load_hh_scales(q):
+            for g in range(PASS_HH):
                 nc.sync.dma_start(
-                    out=pl_ih[32 * q : 32 * q + 4 * PASS_IH, :].bitcast(I32),
-                    in_=ih_s32[:, 4 * q : 4 * q + 4, :],
+                    out=pl_hh[32 * q : 32 * q + 16, SLOT * g : SLOT * (g + 1)].bitcast(I32),
+                    in_=hh_s32[g, :, 4 * q : 4 * q + 4, :],
                 )
-            for q in pair:
-                nc.sync.dma_start(
-                    out=pl_hh[32 * q : 32 * q + 4 * PASS_HH, :].bitcast(I32),
-                    in_=hh_s32[:, 4 * q : 4 * q + 4, :],
-                )
+
+        load_ih_scales(2)
+        load_hh_scales(2)
+        load_ih_scales(3)
+        load_ih_scales(0)
+        load_hh_scales(3)
+        load_ih_scales(1)
 
         last = GROUPS - 1
         half = HS // 2
@@ -93,10 +103,6 @@ def tile_symlstmcell_w_kernel(
             gg = g0 if g0 < PASS_IH else g0 - PASS_IH
             src = words[gg : gg + ng, :, col0 : col0 + ncol, :].rearrange("g p n t -> p g (n t)")
             wt = wpool.tile([P, 4 * HS * last], U32, align_bytes=64, name="wt", tag="wt")
-            if idx == 0:
-                nc.vector.tensor_copy(
-                    out=wt[64:P, 0:1].bitcast(I32), in_=pl_ih[64:P, 0:4].bitcast(I32)
-                )
             nc.sync.dma_start(
                 out=wt[:, 0 : ng * ncol].bitcast(I32).rearrange("p (g n) -> p g n", g=ng),
                 in_=src.bitcast(I32),
@@ -109,7 +115,15 @@ def tile_symlstmcell_w_kernel(
         for idx in range(ahead):
             load_weights(idx)
             if idx == 0:
+                nc.sync.dma_start(
+                    out=brow[0:ROWS, :], in_=bias_ih.rearrange("(r c) -> r c", r=ROWS)
+                )
+                nc.sync.dma_start(
+                    out=brow[ROWS : 2 * ROWS, :], in_=bias_hh.rearrange("(r c) -> r c", r=ROWS)
+                )
                 nc.sync.dma_start(out=c_sb[:], in_=c0)
+            if idx in (1, 2):
+                load_hh_scales(idx - 1)
         issued = [ahead]
 
         def next_load():
@@ -117,7 +131,9 @@ def tile_symlstmcell_w_kernel(
                 load_weights(issued[0])
                 issued[0] = issued[0] + 1
 
-        nc.vector.tensor_tensor(out=pick[:], in0=ident[:, 0:4], in1=ident[:, 4:8], op=ALU.add)
+        nc.vector.tensor_tensor(
+            out=pick[:], in0=ident[:, 0:ROWS], in1=ident[:, ROWS : 2 * ROWS], op=ALU.add
+        )
 
         xw = x_sb[:].bitcast(F32)
         hw = h_sb[:].bitcast(F32)
@@ -153,31 +169,35 @@ def tile_symlstmcell_w_kernel(
                 in_=grp[:, 512 * g0 : 512 * (g0 + ng)],
             )
 
-        for n in range(NCOL // 512):
+        for r in range(ROWS):
             bb = psum.tile([P, 512], F32, name="bb", tag="bank")
-            r, c = divmod(n, 3)
             nc.tensor.matmul(
-                out=bb[:],
+                out=bb[:, 0:PIECE],
                 lhsT=pick[:, r : r + 1].to_broadcast([P, P]),
-                rhs=brow[:, 512 * c : 512 * (c + 1)],
+                rhs=brow[:],
                 start=True,
                 stop=True,
             )
-            if n % 2 == 0:
-                nc.scalar.copy(out=bias_sb[:, 512 * n : 512 * (n + 1)], in_=bb[:])
+            dst = bias_sb[:, PIECE * r : PIECE * (r + 1)]
+            if r % 2 == 0:
+                nc.scalar.copy(out=dst, in_=bb[:, 0:PIECE])
             else:
-                nc.vector.tensor_copy(out=bias_sb[:, 512 * n : 512 * (n + 1)], in_=bb[:])
+                nc.vector.tensor_copy(out=dst, in_=bb[:, 0:PIECE])
 
         def mx_pass(acc_tile, g, col, width):
             wt, at = rhs_of[(g, col // half)]
-            plane = pl_ih if g < PASS_IH else pl_hh
-            k = 4 * (g if g < PASS_IH else g - PASS_IH)
+            if g < PASS_IH:
+                plane = pl_ih[4 * g : P, col : col + width]
+            else:
+                s, c = divmod(col, SLOT)
+                lo = SLOT * (g - PASS_IH) + c
+                plane = pl_hh[4 * s : P, lo : lo + width]
             nc.tensor.matmul_mx(
                 out=acc_tile[:, 0:width],
                 lhsT=xq[:, P * g : P * (g + 1)].bitcast(FP8X4),
                 lhsT_scale=xs[:, P * g : P * (g + 1)],
                 rhs=wt[:, at : at + width].bitcast(FP8X4),
-                rhs_scale=plane[k:P, col : col + width],
+                rhs_scale=plane,
                 start=(g == 0),
                 stop=(g == PASSES - 1),
             )

@@ -216,29 +216,27 @@ def tile_symlstmcell_w_kernel(
                 func=(ACT.Tanh if q == 0 else ACT.Sigmoid),
             )
 
-        def cell(gt, th, j):
+        def gate_products(gt, j, lo, width):
+            unit = slice(HS * j + lo, HS * j + lo + width)
+            at_g, at_i, at_f = (slice(HS * q + lo, HS * q + lo + width) for q in range(3))
             nc.vector.tensor_tensor(
-                out=gt[:, 0:HS], in0=gt[:, 0:HS], in1=gt[:, HS : 2 * HS], op=ALU.mult
+                out=gt[:, at_g], in0=gt[:, at_g], in1=gt[:, at_i], op=ALU.mult
             )
             nc.vector.tensor_tensor(
-                out=gt[:, 2 * HS : 3 * HS],
-                in0=c_sb[:, HS * j : HS * (j + 1)],
-                in1=gt[:, 2 * HS : 3 * HS],
-                op=ALU.mult,
+                out=gt[:, at_f], in0=c_sb[:, unit], in1=gt[:, at_f], op=ALU.mult
             )
-            for s in range(2):
-                lo = half * s
-                nc.vector.tensor_tensor(
-                    out=c1_sb[:, HS * j + lo : HS * j + lo + half],
-                    in0=gt[:, lo : lo + half],
-                    in1=gt[:, 2 * HS + lo : 2 * HS + lo + half],
-                    op=ALU.add,
-                )
-                nc.scalar.activation(
-                    out=th[:, lo : lo + half],
-                    in_=c1_sb[:, HS * j + lo : HS * j + lo + half],
-                    func=ACT.Tanh,
-                )
+
+        def new_cell(gt, th, j, lo, width):
+            unit = slice(HS * j + lo, HS * j + lo + width)
+            nc.vector.tensor_tensor(
+                out=c1_sb[:, unit],
+                in0=gt[:, lo : lo + width],
+                in1=gt[:, 2 * HS + lo : 2 * HS + lo + width],
+                op=ALU.add,
+            )
+            nc.scalar.activation(
+                out=th[:, lo : lo + width], in_=c1_sb[:, unit], func=ACT.Tanh
+            )
 
         def hidden(gt, th, j, lo, width):
             nc.vector.tensor_tensor(
@@ -264,7 +262,9 @@ def tile_symlstmcell_w_kernel(
             th = work.tile([P, HS], F32, name="th", tag="th")
             for q in order:
                 gate(gt, acc[(j, q)][:], j, q, 0, HS)
-            cell(gt, th, j)
+            gate_products(gt, j, 0, HS)
+            for s in range(2):
+                new_cell(gt, th, j, half * s, half)
             for s in range(2):
                 hidden(gt, th, j, half * s, half)
 
@@ -277,9 +277,13 @@ def tile_symlstmcell_w_kernel(
             next_load()
             for q in order[0:3]:
                 mx_pass(acc[(j, q)], g, HS * (4 * j + q), HS)
-        for q in order[0:3]:
-            gate(gt, acc[(j, q)][:], j, q, 0, HS)
-        cell(gt, th, j)
+        for s in range(2):
+            for q in order[0:3]:
+                gate(gt, acc[(j, q)][:, half * s : half * (s + 1)], j, q, half * s, half)
+        for s in range(2):
+            gate_products(gt, j, half * s, half)
+        for s in range(2):
+            new_cell(gt, th, j, half * s, half)
         o_acc = []
         for s in range(2):
             oa = psum.tile([P, 512], F32, name="oa", tag="bank")

@@ -92,8 +92,9 @@ def tile_symlstmcell_w_kernel(
         last = GROUPS - 1
         half = HS // 2
         loads = [(g, 1, 0, 4 * HS * last) for g in range(PASSES)]
-        loads += [(g, 1, 4 * HS * last, 3 * HS) for g in range(PASSES)]
-        loads += [(0, 4, 4 * HS * last + 3 * HS, HS), (4, 2, 4 * HS * last + 3 * HS, HS)]
+        loads += [(g, 1, 4 * HS * last, 3 * HS) for g in range(PASSES - 1)]
+        loads += [(6, 1, 4 * HS * last, 2 * HS), (6, 1, 4 * HS * last + 2 * HS, HS)]
+        loads += [(g, 2, 4 * HS * last + 3 * HS, HS) for g in (0, 2, 4)]
         loads += [(6, 1, 4 * HS * last + 3 * HS + s * half, half) for s in range(2)]
         rhs_of = {}
 

from contextlib import ExitStack

import concourse.mybir as mybir
from concourse.masks import make_identity

F32 = mybir.dt.float32
BF16 = mybir.dt.bfloat16
I32 = mybir.dt.int32
U32 = mybir.dt.uint32
U8 = mybir.dt.uint8
FP8X4 = mybir.dt.float8_e4m3fn_x4
ACT = mybir.ActivationFunctionType
ALU = mybir.AluOpType

P = 128
K_IH = 2048
K_HH = 1536
HS = 512
GROUPS = 3
H = HS * GROUPS
NCOL = 4 * H
PASS_IH = K_IH // 512
PASS_HH = K_HH // 512
PASSES = PASS_IH + PASS_HH
W_BUFS = 7
SLOT = NCOL // 4
ROWS = 16
PIECE = NCOL // ROWS
FLOPS = 2 * P * (K_IH + K_HH) * NCOL


def tile_symlstmcell_w_kernel(
    tc, x, h0, c0, ih_words, ih_scales, hh_words, hh_scales, bias_ih, bias_hh, out_h, out_c
):
    nc = tc.nc
    with ExitStack() as ctx:
        ctx.enter_context(tc.manual_schedule())
        const = ctx.enter_context(tc.tile_pool(name="const", bufs=1))
        wpool = ctx.enter_context(tc.tile_pool(name="wpool", bufs=W_BUFS))
        work = ctx.enter_context(tc.tile_pool(name="work", bufs=2))
        psum = ctx.enter_context(tc.psum_pool(name="psum", bufs=8))

        x_sb = const.tile([P, K_IH], BF16)
        h_sb = const.tile([P, K_HH], BF16)
        c_sb = const.tile([P, H], BF16)
        ident = const.tile([P, P], F32)
        pick = const.tile([P, ROWS], BF16)
        brow = const.tile([P, PIECE], BF16)
        warm = const.tile([P, 1], F32)
        bias_sb = const.tile([P, NCOL], F32)
        pl_ih = const.tile([P, NCOL], U8, align_bytes=64)
        pl_hh = const.tile([P, PASS_HH * SLOT], U8, align_bytes=64)
        grp = const.tile([P, PASSES * 512], BF16, align_bytes=64)
        xq = const.tile([P, PASSES * P], U32, align_bytes=64)
        xs = const.tile([P, PASSES * P], U8, align_bytes=64)
        c1_sb = const.tile([P, H], F32)
        h1_sb = const.tile([P, H], F32)

        nc.vector.memset(pl_ih[:].bitcast(I32), 0)
        nc.vector.memset(pl_hh[:].bitcast(I32), 0)
        nc.vector.memset(brow[:].bitcast(I32), 0)
        nc.vector.memset(warm[:], 0.0)
        make_identity(nc, ident[:])

        nc.sync.dma_start(out=x_sb[:], in_=x)
        nc.sync.dma_start(out=h_sb[:], in_=h0)
        nc.scalar.activation(out=warm[:], in_=warm[:], func=ACT.Sigmoid)

        ih_s32 = ih_scales.bitcast(I32)
        hh_s32 = hh_scales.rearrange("g q (s c) -> g s q c", s=4).bitcast(I32)

        def load_ih_scales(q):
            nc.sync.dma_start(
                out=pl_ih[32 * q : 32 * q + 4 * PASS_IH, :].bitcast(I32),
                in_=ih_s32[:, 4 * q : 4 * q + 4, :],
            )

        def load_hh_scales(q):
            for g in range(PASS_HH):
                nc.sync.dma_start(
                    out=pl_hh[32 * q : 32 * q + 16, SLOT * g : SLOT * (g + 1)].bitcast(I32),
                    in_=hh_s32[g, :, 4 * q : 4 * q + 4, :],
                )

        load_ih_scales(2)
        load_hh_scales(2)
        load_ih_scales(3)
        load_ih_scales(0)
        load_hh_scales(3)
        load_ih_scales(1)

        last = GROUPS - 1
        half = HS // 2
        loads = [(g, 1, 0, 4 * HS * last) for g in range(PASSES)]
        loads += [(g, 1, 4 * HS * last, 3 * HS) for g in range(PASSES - 1)]
        loads += [(6, 1, 4 * HS * last, 2 * HS), (6, 1, 4 * HS * last + 2 * HS, HS)]
        loads += [(g, 2, 4 * HS * last + 3 * HS, HS) for g in (0, 2, 4)]
        loads += [(6, 1, 4 * HS * last + 3 * HS + s * half, half) for s in range(2)]
        rhs_of = {}

        def load_weights(idx):
            g0, ng, col0, ncol = loads[idx]
            words = ih_words if g0 < PASS_IH else hh_words
            gg = g0 if g0 < PASS_IH else g0 - PASS_IH
            src = words[gg : gg + ng, :, col0 : col0 + ncol, :].rearrange("g p n t -> p g (n t)")
            wt = wpool.tile([P, 4 * HS * last], U32, align_bytes=64, name="wt", tag="wt")
            nc.sync.dma_start(
                out=wt[:, 0 : ng * ncol].bitcast(I32).rearrange("p (g n) -> p g n", g=ng),
                in_=src.bitcast(I32),
            )
            for a in range(ng):
                for c in range(ncol // half):
                    rhs_of[(g0 + a, col0 // half + c)] = (wt, a * ncol + c * half)

        ahead = W_BUFS - 1
        for idx in range(ahead):
            load_weights(idx)
            if idx == 0:
                nc.sync.dma_start(
                    out=brow[0:ROWS, :], in_=bias_ih.rearrange("(r c) -> r c", r=ROWS)
                )
                nc.sync.dma_start(
                    out=brow[ROWS : 2 * ROWS, :], in_=bias_hh.rearrange("(r c) -> r c", r=ROWS)
                )
                nc.sync.dma_start(out=c_sb[:], in_=c0)
            if idx in (1, 2):
                load_hh_scales(idx - 1)
        issued = [ahead]

        def next_load():
            if issued[0] < len(loads):
                load_weights(issued[0])
                issued[0] = issued[0] + 1

        nc.vector.tensor_tensor(
            out=pick[:], in0=ident[:, 0:ROWS], in1=ident[:, ROWS : 2 * ROWS], op=ALU.add
        )

        xw = x_sb[:].bitcast(F32)
        hw = h_sb[:].bitcast(F32)
        grpw = grp[:].bitcast(F32)
        banks = [(0, 2), (2, 2), (4, 2), (6, 1)]
        t_tiles = []
        for g0, ng in banks:
            tt = psum.tile([P, 512], F32, name="tt", tag="bank")
            for gl in range(ng):
                g = g0 + gl
                src = xw if g < PASS_IH else hw
                gg = g if g < PASS_IH else g - PASS_IH
                for u in range(2):
                    nc.tensor.transpose(
                        out=tt[:, 128 * (2 * gl + u) : 128 * (2 * gl + u + 1)],
                        in_=src[:, 256 * gg + u : 256 * (gg + 1) : 2],
                        identity=ident[:],
                    )
            t_tiles.append(tt)
        for b, (g0, ng) in enumerate(banks):
            dst = grpw[:, 256 * g0 : 256 * (g0 + ng)].rearrange(
                "p (a m u) -> p a m u", a=ng, m=P, u=2
            )
            srcv = t_tiles[b][:, 0 : 256 * ng].rearrange("p (a u m) -> p a m u", a=ng, u=2, m=P)
            if b % 2 == 0:
                nc.vector.tensor_copy(out=dst, in_=srcv)
            else:
                nc.scalar.copy(out=dst, in_=srcv)
        for g0, ng in banks:
            nc.vector.quantize_mx(
                out=xq[:, P * g0 : P * (g0 + ng)].bitcast(FP8X4),
                scales=xs[:, P * g0 : P * (g0 + ng)],
                in_=grp[:, 512 * g0 : 512 * (g0 + ng)],
            )

        for r in range(ROWS):
            bb = psum.tile([P, 512], F32, name="bb", tag="bank")
            nc.tensor.matmul(
                out=bb[:, 0:PIECE],
                lhsT=pick[:, r : r + 1].to_broadcast([P, P]),
                rhs=brow[:],
                start=True,
                stop=True,
            )
            dst = bias_sb[:, PIECE * r : PIECE * (r + 1)]
            if r % 2 == 0:
                nc.scalar.copy(out=dst, in_=bb[:, 0:PIECE])
            else:
                nc.vector.tensor_copy(out=dst, in_=bb[:, 0:PIECE])

        def mx_pass(acc_tile, g, col, width):
            wt, at = rhs_of[(g, col // half)]
            if g < PASS_IH:
                plane = pl_ih[4 * g : P, col : col + width]
            else:
                s, c = divmod(col, SLOT)
                lo = SLOT * (g - PASS_IH) + c
                plane = pl_hh[4 * s : P, lo : lo + width]
            nc.tensor.matmul_mx(
                out=acc_tile[:, 0:width],
                lhsT=xq[:, P * g : P * (g + 1)].bitcast(FP8X4),
                lhsT_scale=xs[:, P * g : P * (g + 1)],
                rhs=wt[:, at : at + width].bitcast(FP8X4),
                rhs_scale=plane,
                start=(g == 0),
                stop=(g == PASSES - 1),
            )

        def gate(gt, sums, j, q, lo, width):
            col = 4 * HS * j + HS * q + lo
            nc.vector.tensor_tensor(
                out=gt[:, HS * q + lo : HS * q + lo + width],
                in0=sums,
                in1=bias_sb[:, col : col + width],
                op=ALU.add,
            )
            nc.scalar.activation(
                out=gt[:, HS * q + lo : HS * q + lo + width],
                in_=gt[:, HS * q + lo : HS * q + lo + width],
                func=(ACT.Tanh if q == 0 else ACT.Sigmoid),
            )

        def gate_products(gt, j, lo, width):
            unit = slice(HS * j + lo, HS * j + lo + width)
            at_g, at_i, at_f = (slice(HS * q + lo, HS * q + lo + width) for q in range(3))
            nc.vector.tensor_tensor(
                out=gt[:, at_g], in0=gt[:, at_g], in1=gt[:, at_i], op=ALU.mult
            )
            nc.vector.tensor_tensor(
                out=gt[:, at_f], in0=c_sb[:, unit], in1=gt[:, at_f], op=ALU.mult
            )

        def new_cell(gt, th, j, lo, width):
            unit = slice(HS * j + lo, HS * j + lo + width)
            nc.vector.tensor_tensor(
                out=c1_sb[:, unit],
                in0=gt[:, lo : lo + width],
                in1=gt[:, 2 * HS + lo : 2 * HS + lo + width],
                op=ALU.add,
            )
            nc.scalar.activation(
                out=th[:, lo : lo + width], in_=c1_sb[:, unit], func=ACT.Tanh
            )

        def hidden(gt, th, j, lo, width):
            nc.vector.tensor_tensor(
                out=h1_sb[:, HS * j + lo : HS * j + lo + width],
                in0=th[:, lo : lo + width],
                in1=gt[:, 3 * HS + lo : 3 * HS + lo + width],
                op=ALU.mult,
            )

        order = (1, 0, 2, 3)
        acc = {}

        for j in range(last):
            for q in order:
                acc[(j, q)] = psum.tile([P, 512], F32, name="acc", tag="bank")
        for g in range(PASSES):
            next_load()
            for j in range(last):
                for q in order:
                    mx_pass(acc[(j, q)], g, HS * (4 * j + q), HS)
        for j in range(last):
            gt = work.tile([P, 4 * HS], F32, name="gt", tag="gt")
            th = work.tile([P, HS], F32, name="th", tag="th")
            for q in order:
                gate(gt, acc[(j, q)][:], j, q, 0, HS)
            gate_products(gt, j, 0, HS)
            for s in range(2):
                new_cell(gt, th, j, half * s, half)
            for s in range(2):
                hidden(gt, th, j, half * s, half)

        j = last
        for q in order[0:3]:
            acc[(j, q)] = psum.tile([P, 512], F32, name="acc", tag="bank")
        gt = work.tile([P, 4 * HS], F32, name="gt", tag="gt")
        th = work.tile([P, HS], F32, name="th", tag="th")
        for g in range(PASSES):
            next_load()
            for q in order[0:3]:
                mx_pass(acc[(j, q)], g, HS * (4 * j + q), HS)
        for s in range(2):
            for q in order[0:3]:
                gate(gt, acc[(j, q)][:, half * s : half * (s + 1)], j, q, half * s, half)
        for s in range(2):
            gate_products(gt, j, half * s, half)
        for s in range(2):
            new_cell(gt, th, j, half * s, half)
        o_acc = []
        for s in range(2):
            oa = psum.tile([P, 512], F32, name="oa", tag="bank")
            o_acc.append(oa)
        for g in range(PASSES):
            for s in range(2):
                mx_pass(o_acc[s], g, HS * (4 * j + 3) + half * s, half)
        for s in range(2):
            gate(gt, o_acc[s][:, 0:half], j, 3, half * s, half)
        for s in range(2):
            hidden(gt, th, j, half * s, half)

        nc.sync.dma_start(out=out_c[:, 0 : 2 * HS], in_=c1_sb[:, 0 : 2 * HS])
        nc.sync.dma_start(out=out_h[:, 0 : 2 * HS], in_=h1_sb[:, 0 : 2 * HS])
        nc.sync.dma_start(out=out_c[:, 2 * HS : H], in_=c1_sb[:, 2 * HS : H])
        for s in range(2):
            lo = HS * j + half * s
            nc.sync.dma_start(out=out_h[:, lo : lo + half], in_=h1_sb[:, lo : lo + half])
